import numpy as np
import ml_dtypes


def mxq(x, axis, fmt="e4m3"):
    dtype, down = {"e4m3": (ml_dtypes.float8_e4m3fn, 7), "e5m2": (ml_dtypes.float8_e5m2, 14)}[fmt]
    v = np.moveaxis(np.asarray(x, np.float32).astype(ml_dtypes.bfloat16).astype(np.float64), axis, -1)
    blocks = v.reshape(v.shape[:-1] + (-1, 32))
    amax = np.abs(blocks).max(-1, keepdims=True)
    byte = np.maximum(np.where(amax > 0, np.frexp(amax)[1] - 1 + 127, 0) - down, 1)
    scale = np.exp2(byte - 127.0)
    codes = (blocks / scale).astype(np.float32).astype(dtype).astype(np.float64)
    return np.moveaxis((codes * scale).reshape(v.shape), -1, axis)


WIDE = False


def mx_kscale(k):
    if not WIDE:
        return np.ones(k)
    levels = np.array([30, -30])
    if k % 512:
        return np.exp2(np.random.permutation(np.resize(levels, k // 32))).repeat(32)
    a = np.empty((k // 512, 16))
    for p in range(k // 512):
        a[p, :8] = np.random.permutation(np.resize(levels, 8))
        for g in range(8):
            far = levels[np.abs(levels - a[p, g]) >= 10]
            a[p, g + 8] = far[np.random.randint(len(far))]
    return np.exp2(a.ravel()).repeat(32)


BF16 = ml_dtypes.bfloat16


def bf(x):
    return np.asarray(x, np.float32).astype(BF16)


def f64(x):
    return np.asarray(x).astype(np.float64)


B, N1, N2, D, H, DH = 4, 384, 128, 1024, 8, 128
E = H * DH


def rope_tables(n, d):
    inv = 1.0 / (10000.0 ** (np.arange(0, d, 2) / d))
    ang = np.outer(np.arange(n), inv)
    return np.repeat(np.cos(ang), 2, axis=-1), np.repeat(np.sin(ang), 2, axis=-1)


def apply_rope(x, cos, sin):
    xr = x.reshape(x.shape[:-1] + (-1, 2))
    x_real, x_imag = xr[..., 0], xr[..., 1]
    x_rot = np.stack([-x_imag, x_real], axis=-1).reshape(x.shape)
    return x * cos[None, None] + x_rot * sin[None, None]


def split_heads(t):
    b, n, _ = t.shape
    return t.reshape(b, n, H, DH).transpose(0, 2, 1, 3)


def setup_inputs():
    s1, s2 = mx_kscale(D), mx_kscale(D)
    cos1, sin1 = rope_tables(N1, DH)
    cos2, sin2 = rope_tables(N2, DH)

    def w(s):
        return bf(np.random.standard_normal((D, E)) * 1.4 / np.sqrt(D) / s[:, None])

    def b():
        return bf(np.random.standard_normal(E) * 0.3)

    return {"x_1": bf(np.random.standard_normal((B, N1, D)) * s1), "x_2": bf(np.random.standard_normal((B, N2, D)) * s2),
            "cos1": bf(cos1), "sin1": bf(sin1), "cos2": bf(cos2), "sin2": bf(sin2),
            "wq1": w(s1), "bq1": b(), "wk1": w(s1), "bk1": b(),
            "wq2": w(s2), "bq2": b(), "wk2": w(s2), "bk2": b()}


def reference(x_1, x_2, cos1, sin1, cos2, sin2, wq1, bq1, wk1, bk1, wq2, bq2, wk2, bk2):
    x1q = mxq(f64(x_1), 2, "e5m2")
    x2q = mxq(f64(x_2), 2, "e5m2")
    q = np.concatenate([(x1q @ mxq(f64(wq1), 0, "e5m2")) + f64(bq1),
                        (x2q @ mxq(f64(wq2), 0, "e5m2")) + f64(bq2)], axis=1)
    k = np.concatenate([(x1q @ mxq(f64(wk1), 0, "e5m2")) + f64(bk1),
                        (x2q @ mxq(f64(wk2), 0, "e5m2")) + f64(bk2)], axis=1)
    q, k = split_heads(q), split_heads(k)
    q = q * (DH ** -0.5)
    cos = np.concatenate([f64(cos1), f64(cos2)], axis=0)
    sin = np.concatenate([f64(sin1), f64(sin2)], axis=0)
    return apply_rope(q, cos, sin), apply_rope(k, cos, sin)

@@ -1,0 +1,329 @@
+from contextlib import ExitStack
+
+import concourse.mybir as mybir
+from concourse.masks import make_identity
+
+B, N1, N2, D, H, DH = 4, 384, 128, 1024, 8, 128
+E = H * DH
+FLOPS = 2 * 2 * B * (N1 + N2) * D * E
+
+F32 = mybir.dt.float32
+BF16 = mybir.dt.bfloat16
+U32 = mybir.dt.uint32
+U8 = mybir.dt.uint8
+FP8X4 = mybir.dt.float8_e5m2_x4
+ALU = mybir.AluOpType
+ACT = mybir.ActivationFunctionType
+
+P = 128
+PACK = 4
+K_PASS = P * PACK
+PASSES = D // K_PASS
+GROUPS = 4
+NTOK = B * P
+PAIR = 2 * DH
+HALF = 2 * PAIR
+ROUNDS = 4
+UNITS_PER_ROUND = 2 * GROUPS
+UNITS = ROUNDS * UNITS_PER_ROUND
+Q_SCALE = DH ** -0.5
+
+
+def tile_dualmultiheadattention_pa_kernel(
+    tc, x_1, x_2, cos1, sin1, cos2, sin2, wq1, bq1, wk1, bk1, wq2, bq2, wk2, bk2, out_0, out_1
+):
+    nc = tc.nc
+    weights = [wq1, wq2, wk1, wk2]
+    biases = [bq1, bq2, bk1, bk2]
+    outs = [out_0, out_1]
+    x1_rows = x_1.rearrange("b (p i) k -> i p b k", i=3)
+    x_rows = [x1_rows[0], x1_rows[1], x1_rows[2], x_2.rearrange("b p k -> p b k")]
+
+    with ExitStack() as ctx:
+        keep = ctx.enter_context(tc.tile_pool(name="keep", bufs=1))
+        flow = ctx.enter_context(tc.tile_pool(name="flow", bufs=2))
+        psum = ctx.enter_context(tc.psum_pool(name="psum", bufs=4))
+        ctx.enter_context(tc.manual_schedule())
+
+        ident_f32 = keep.tile([P, P], F32)
+        ident_bf16 = keep.tile([P, P], BF16)
+        cos_raw = keep.tile([P, GROUPS, DH], BF16)
+        sin_raw = keep.tile([P, GROUPS, DH], BF16)
+        bias_rows = keep.tile([P, PAIR], BF16)
+        bias_cols = keep.tile([P, 2, 16], F32)
+        tab_rows = keep.tile([P, GROUPS, 2, 2, 2, 64], BF16)
+        tabs = keep.tile([P, GROUPS, 2, 2, P], BF16)
+        x_codes = keep.tile([P, GROUPS, PASSES, NTOK], U32, align_bytes=64)
+        x_scales = keep.tile([P, GROUPS, PASSES, NTOK], U8, align_bytes=64)
+
+        x_raw, w_raw, x_grouped, w_grouped, w_codes, w_scales = {}, {}, {}, {}, {}, {}
+        acc, prods, sums, stage = {}, {}, {}, {}
+
+        def load_x(i):
+            for sp in range(2):
+                t = keep.tile([P, 2, D], BF16, name="x_raw_%d_%d" % (i, sp))
+                nc.sync.dma_start(out=t[:], in_=x_rows[i][:, 2 * sp : 2 * sp + 2, :])
+                x_raw[i, sp] = t
+
+        def load_w(m, half):
+            for g in range(PASSES):
+                t = flow.tile([P, PACK, HALF], BF16, name="w_raw", bufs=8)
+                rows = weights[m][g * K_PASS : (g + 1) * K_PASS, half * HALF : (half + 1) * HALF]
+                nc.sync.dma_start(out=t[:], in_=rows.rearrange("(p t) c -> p t c", t=PACK))
+                w_raw[m, half, g] = t
+
+        def turn_x(i, sp, g, copy):
+            if (sp, g) == (0, 0):
+                x_grouped[i] = flow.tile([P, PASSES * NTOK * PACK], BF16, name="x_grouped", align_bytes=64)
+            words = x_raw[i, sp][:].rearrange("p s k -> p (s k)").bitcast(F32)
+            bank = psum.tile([P, 2, 2, P], F32, name="turned")
+            for s in range(2):
+                w0 = s * (D // 2) + g * (K_PASS // 2)
+                for u in range(2):
+                    nc.tensor.transpose(bank[:, s, u, :], words[:, w0 + u : w0 + K_PASS // 2 : 2], ident_f32[:])
+            o0 = g * 2 * NTOK + sp * NTOK
+            dst = x_grouped[i][:].bitcast(F32)[:, o0 : o0 + NTOK]
+            copy(out=dst.rearrange("p (s r u) -> p s r u", s=2, u=2), in_=bank[:].rearrange("p s u r -> p s r u"))
+
+        def quantize_x(i, g0, g1):
+            nc.vector.quantize_mx(
+                out=x_codes[:, i, g0:g1, :].rearrange("p g n -> p (g n)").bitcast(FP8X4),
+                scales=x_scales[:, i, g0:g1, :].rearrange("p g n -> p (g n)"),
+                in_=x_grouped[i][:, g0 * NTOK * PACK : g1 * NTOK * PACK],
+            )
+
+        def group_w(m, pair, g, copy):
+            if g == 0:
+                w_grouped[m, pair] = flow.tile([P, PASSES, 2, P, PACK], BF16, name="w_grouped", bufs=4, align_bytes=64)
+            c0 = (pair % 2) * PAIR
+            src = w_raw[m, pair // 2, g][:, :, c0 : c0 + PAIR]
+            copy(out=w_grouped[m, pair][:, g], in_=src.rearrange("p t (m e) -> p e m t", e=2))
+
+        def quantize_w(m, pair):
+            codes = flow.tile([P, PASSES, 2, P], U32, name="w_codes", bufs=6, align_bytes=64)
+            scales = flow.tile([P, PASSES, 2, P], U8, name="w_scales", bufs=6, align_bytes=64)
+            nc.vector.quantize_mx(
+                out=codes[:].rearrange("p g e m -> p (g e m)").bitcast(FP8X4),
+                scales=scales[:].rearrange("p g e m -> p (g e m)"),
+                in_=w_grouped[m, pair][:].rearrange("p g e m t -> p (g e m t)"),
+            )
+            w_codes[m, pair], w_scales[m, pair] = codes, scales
+
+        def spread_tables(i0, i1):
+            n = i1 - i0
+            cos_e = cos_raw[:, i0:i1, :].rearrange("p i (j e) -> p i e j", e=2)
+            sin_e = sin_raw[:, i0:i1, :].rearrange("p i (j e) -> p i e j", e=2)
+            nc.vector.tensor_copy(
+                out=tab_rows[:, i0:i1, 0], in_=cos_e.unsqueeze(3).to_broadcast([P, n, 2, 2, 64])
+            )
+            nc.vector.tensor_copy(
+                out=tab_rows[:, i0:i1, 1, 0], in_=sin_e[:, :, 1:2, :].to_broadcast([P, n, 2, 64])
+            )
+            nc.vector.tensor_scalar(
+                out=tab_rows[:, i0:i1, 1, 1],
+                in0=sin_e[:, :, 0:1, :].to_broadcast([P, n, 2, 64]),
+                scalar1=-1.0,
+                scalar2=None,
+                op0=ALU.mult,
+            )
+
+        def turn_tables(i):
+            bank = psum.tile([P, 2, 2, P], BF16, name="turned")
+            for cs in range(2):
+                for e in range(2):
+                    src = tab_rows[:, i, cs, e].rearrange("p h j -> p (h j)")
+                    nc.tensor.transpose(bank[:, cs, e, :], src, ident_bf16[:])
+            nc.scalar.copy(out=tabs[:, i], in_=bank[:])
+
+        def turn_bias():
+            bank = psum.tile([P, 2, P], BF16, name="turned")
+            for e in range(2):
+                nc.tensor.transpose(bank[:, e, :], bias_rows[:, e:PAIR:2], ident_bf16[:])
+            nc.scalar.copy(out=bias_cols[:], in_=bank[:, :, 0:16])
+
+        def unit(u):
+            r, v = divmod(u, UNITS_PER_ROUND)
+            i, pp = divmod(v, 2)
+            qk = r // 2
+            return qk, 2 * qk + (1 if i == GROUPS - 1 else 0), 2 * (r % 2) + pp, i
+
+        def multiply(u):
+            qk, m, pair, i = unit(u)
+            for e in range(2):
+                bank = psum.tile([P, B, P], F32, name="acc")
+                for g in range(PASSES):
+                    nc.tensor.matmul_mx(
+                        out=bank[:].rearrange("p b n -> p (b n)"),
+                        lhsT=w_codes[m, pair][:, g, e, :].bitcast(FP8X4),
+                        lhsT_scale=w_scales[m, pair][:, g, e, :],
+                        rhs=x_codes[:, i, g, :].bitcast(FP8X4),
+                        rhs_scale=x_scales[:, i, g, :],
+                        start=(g == 0),
+                        stop=(g == PASSES - 1),
+                    )
+                acc[u, e] = bank
+
+        def rotate(u, e):
+            qk, m, pair, i = unit(u)
+            if e == 0:
+                prods[u] = flow.tile([P, 2, 2, B, P], F32, name="prods", bufs=4)
+            col = 4 * m + pair
+            for cs in range(2):
+                nc.vector.scalar_tensor_tensor(
+                    out=prods[u][:, cs, e if cs == 0 else 1 - e],
+                    in0=acc[u, e][:],
+                    scalar=bias_cols[:, e, col : col + 1],
+                    in1=tabs[:, i, cs, e, :].unsqueeze(1).to_broadcast([P, B, P]),
+                    op0=ALU.add,
+                    op1=ALU.mult,
+                )
+
+        def add_products(u):
+            sums[u] = flow.tile([P, 2, B, P], F32, name="sums")
+            nc.gpsimd.tensor_tensor(
+                out=sums[u][:].rearrange("p e b n -> p (e b n)"),
+                in0=prods[u][:, 0].rearrange("p e b n -> p (e b n)"),
+                in1=prods[u][:, 1].rearrange("p e b n -> p (e b n)"),
+                op=ALU.add,
+            )
+
+        def turn_out(u):
+            qk, m, pair, i = unit(u)
+            if i == 0:
+                stage[m, pair] = flow.tile([P, 2, B, 3, DH], F32, name="stage1", bufs=3)
+            if i == GROUPS - 1:
+                stage[m, pair] = flow.tile([P, 2, B, 1, DH], F32, name="stage2")
+            for hb in range(2):
+                bank = psum.tile([P, 2, 2, 2, 64], F32, name="turned")
+                for s in range(2):
+                    b = 2 * hb + s
+                    for e in range(2):
+                        dst = bank[:, s, :, e, :]
+                        if u % 2 == 0:
+                            nc.tensor.transpose(dst, sums[u][:, e, b, :], ident_f32[:])
+                        else:
+                            for cs in range(2):
+                                nc.tensor.matmul(
+                                    dst,
+                                    lhsT=prods[u][:, cs, e, b, :],
+                                    rhs=ident_f32[:],
+                                    start=(cs == 0),
+                                    stop=(cs == 1),
+                                    is_transpose=True,
+                                )
+                dst = stage[m, pair][:, :, 2 * hb : 2 * hb + 2, i % 3, :].rearrange("p h s (j e) -> p s h j e", e=2)
+                src = bank[:].rearrange("p s h e j -> p s h j e")
+                if qk == 0:
+                    nc.scalar.activation(out=dst, in_=src, func=ACT.Copy, scale=Q_SCALE)
+                else:
+                    nc.scalar.copy(out=dst, in_=src)
+
+        def store(u):
+            qk, m, pair, i = unit(u)
+            last_round = u >= UNITS - UNITS_PER_ROUND
+            if i == 3:
+                i0, i1 = 0, 1
+            elif i == 2:
+                i0, i1 = (2, 3) if last_round else (0, 3)
+            elif i == 1 and last_round:
+                i0, i1 = 0, 2
+            else:
+                return
+            for hh in range(2):
+                head = outs[qk][:, 2 * pair + hh]
+                if i == 3:
+                    rows = head[:, N1:, :].rearrange("b (p i) c -> p b i c", i=1)
+                else:
+                    rows = head[:, :N1, :].rearrange("b (p i) c -> p b i c", i=3)
+                nc.sync.dma_start(
+                    out=rows[:, :, i0:i1, :].rearrange("p b i c -> p b (i c)"),
+                    in_=stage[m, pair][:, hh, :, i0:i1, :].rearrange("p b i c -> p b (i c)"),
+                )
+
+        v_copy, s_copy = nc.vector.tensor_copy, nc.scalar.copy
+
+        load_x(0)
+        load_w(0, 0)
+        load_x(1)
+        load_w(1, 0)
+        load_x(2)
+        load_x(3)
+        load_w(0, 1)
+        load_w(1, 1)
+        nc.vector.memset(bias_rows[:], 0.0)
+        make_identity(nc, ident_f32[:])
+        nc.gpsimd.dma_start(out=cos_raw[:, 0:3, :], in_=cos1.rearrange("(p i) c -> p i c", i=3))
+        nc.gpsimd.dma_start(out=sin_raw[:, 0:3, :], in_=sin1.rearrange("(p i) c -> p i c", i=3))
+        for m in range(4):
+            nc.gpsimd.dma_start(out=bias_rows[4 * m : 4 * m + 4, :], in_=biases[m].rearrange("(r c) -> r c", c=PAIR))
+        nc.gpsimd.dma_start(out=cos_raw[:, 3, :], in_=cos2)
+        nc.gpsimd.dma_start(out=sin_raw[:, 3, :], in_=sin2)
+        nc.vector.tensor_copy(out=ident_bf16[:], in_=ident_f32[:])
+
+        turn_x(0, 0, 0, v_copy)
+        turn_x(0, 0, 1, s_copy)
+        spread_tables(0, 1)
+        turn_x(0, 1, 0, s_copy)
+        group_w(0, 0, 0, v_copy)
+        turn_x(0, 1, 1, s_copy)
+        group_w(0, 0, 1, v_copy)
+        turn_tables(0)
+        turn_bias()
+        quantize_x(0, 0, 1)
+        quantize_w(0, 0)
+        quantize_x(0, 1, 2)
+        group_w(0, 1, 0, s_copy)
+        group_w(0, 1, 1, v_copy)
+        turn_x(1, 0, 0, s_copy)
+        turn_x(1, 0, 1, s_copy)
+        multiply(0)
+        quantize_w(0, 1)
+
+        later = []
+        for r in range(ROUNDS):
+            for v in (6, 7, 8, 9):
+                if r * UNITS_PER_ROUND + v < UNITS:
+                    later.append(unit(r * UNITS_PER_ROUND + v)[1:3])
+        pieces = [(m, pair, g) for (m, pair) in later for g in range(PASSES)]
+        pieces_done, pairs_done = 0, 0
+
+        for u in range(UNITS + 2):
+            if u == 0:
+                turn_x(1, 1, 0, s_copy)
+                turn_x(1, 1, 1, s_copy)
+            if u + 1 < UNITS:
+                multiply(u + 1)
+            if u == 4:
+                load_w(2, 0)
+                load_w(3, 0)
+            if u == 12:
+                load_w(2, 1)
+                load_w(3, 1)
+            if u >= 1 and (u - 1) % 2 == 0 and u - 1 < UNITS:
+                add_products(u - 1)
+            if u < UNITS:
+                rotate(u, 0)
+                if u in (2, 4):
+                    quantize_x(u // 2 + 1, 0, PASSES)
+                for n in range({2: 1, 4: 1, 6: 2}.get(u % UNITS_PER_ROUND, 0)):
+                    if pairs_done < len(later):
+                        quantize_w(*later[pairs_done])
+                        pairs_done += 1
+                rotate(u, 1)
+            if u == 0:
+                quantize_x(1, 0, PASSES)
+                spread_tables(1, GROUPS)
+            if u >= 2:
+                turn_out(u - 2)
+                store(u - 2)
+            if u == 1:
+                for i in range(1, GROUPS):
+                    turn_tables(i)
+            if u in (1, 3):
+                for sp in range(2):
+                    for g in range(PASSES):
+                        turn_x((u + 3) // 2, sp, g, s_copy)
+            for n in range(2 if u in (2, 4) else 1):
+                if pieces_done < len(pieces):
+                    group_w(*pieces[pieces_done], s_copy)
+                    pieces_done += 1

@@ -19,14 +19,21 @@ P = 128
 PACK = 4
 K_PASS = P * PACK
 PASSES = D // K_PASS
-GROUPS = 4
+GROUPS1 = N1 // P
+GROUPS = GROUPS1 + 1
 NTOK = B * P
 PAIR = 2 * DH
-HALF = 2 * PAIR
-ROUNDS = 4
-UNITS_PER_ROUND = 2 * GROUPS
-UNITS = ROUNDS * UNITS_PER_ROUND
+PAIRS = H // 2
+HALF_DH = DH // 2
+WQ1, WQ2, WK1, WK2 = range(4)
 Q_SCALE = DH ** -0.5
+
+GROUP_W_SLOT = 2
+QUANTIZE_W_LAG = 2
+X2_SLOT = 1
+X3_SLOT = 7
+QUANTIZE_X_LAG = 2
+TABLE_LEAD = 2
 
 
 def tile_dualmultiheadattention_pa_kernel(
@@ -35,9 +42,20 @@ def tile_dualmultiheadattention_pa_kernel(
     nc = tc.nc
     weights = [wq1, wq2, wk1, wk2]
     biases = [bq1, bq2, bk1, bk2]
-    outs = [out_0, out_1]
-    x1_rows = x_1.rearrange("b (p i) k -> i p b k", i=3)
-    x_rows = [x1_rows[0], x1_rows[1], x1_rows[2], x_2.rearrange("b p k -> p b k")]
+    outs = [out_0, out_0, out_1, out_1]
+    x1_rows = x_1.rearrange("b (p i) k -> i p b k", i=GROUPS1)
+    x_rows = [x1_rows[i] for i in range(GROUPS1)] + [x_2.rearrange("b p k -> p b k")]
+
+    units = [(WQ1, pair, i) for i in range(GROUPS1) for pair in range(PAIRS)]
+    for half, weight2 in enumerate((WQ2, WK2)):
+        units += [(WK1, 2 * half + n, i) for n in range(2) for i in range(GROUPS1)]
+        units += [(weight2, pair, GROUPS1) for pair in range(PAIRS)]
+    last = len(units) - 1
+    later_pairs = []
+    for m, pair, i in units:
+        if m != WQ1 and (m, pair) not in later_pairs:
+            later_pairs.append((m, pair))
+    later_passes = [(m, pair, g) for m, pair in later_pairs for g in range(PASSES)]
 
     with ExitStack() as ctx:
         keep = ctx.enter_context(tc.tile_pool(name="keep", bufs=1))
@@ -50,78 +68,77 @@ def tile_dualmultiheadattention_pa_kernel(
         cos_raw = keep.tile([P, GROUPS, DH], BF16)
         sin_raw = keep.tile([P, GROUPS, DH], BF16)
         bias_rows = keep.tile([P, PAIR], BF16)
-        bias_cols = keep.tile([P, 2, 16], F32)
-        tab_rows = keep.tile([P, GROUPS, 2, 2, 2, 64], BF16)
-        tabs = keep.tile([P, GROUPS, 2, 2, P], BF16)
+        bias_cols = keep.tile([P, 2, len(weights) * PAIRS], F32)
+        table_rows = keep.tile([P, GROUPS, 2, 2, 2, HALF_DH], BF16)
+        tables = keep.tile([P, GROUPS, 2, 2, P], BF16)
         x_codes = keep.tile([P, GROUPS, PASSES, NTOK], U32, align_bytes=64)
         x_scales = keep.tile([P, GROUPS, PASSES, NTOK], U8, align_bytes=64)
 
-        x_raw, w_raw, x_grouped, w_grouped, w_codes, w_scales = {}, {}, {}, {}, {}, {}
-        acc, prods, sums, stage = {}, {}, {}, {}
+        x_raw, x_grouped, w_raw, w_grouped, w_codes, w_scales = {}, {}, {}, {}, {}, {}
+        sums, products, even_added, turned, staged = {}, {}, {}, {}, {}
 
-        def load_x(i):
-            for sp in range(2):
-                t = keep.tile([P, 2, D], BF16, name="x_raw_%d_%d" % (i, sp))
-                nc.sync.dma_start(out=t[:], in_=x_rows[i][:, 2 * sp : 2 * sp + 2, :])
-                x_raw[i, sp] = t
+        def load_x(i, hb):
+            t = flow.tile([P, 2, D], BF16, name="raw", bufs=8)
+            nc.sync.dma_start(out=t[:], in_=x_rows[i][:, 2 * hb : 2 * hb + 2, :])
+            x_raw[i, hb] = t
 
-        def load_w(m, half):
+        def load_w(m, pair0, pairs, tag):
             for g in range(PASSES):
-                t = flow.tile([P, PACK, HALF], BF16, name="w_raw", bufs=8)
-                rows = weights[m][g * K_PASS : (g + 1) * K_PASS, half * HALF : (half + 1) * HALF]
-                nc.sync.dma_start(out=t[:], in_=rows.rearrange("(p t) c -> p t c", t=PACK))
-                w_raw[m, half, g] = t
+                t = flow.tile([P, PACK, pairs, PAIR], BF16, name=tag, bufs=8)
+                rows = weights[m][g * K_PASS : (g + 1) * K_PASS, pair0 * PAIR : (pair0 + pairs) * PAIR]
+                nc.sync.dma_start(
+                    out=t[:].rearrange("p t n c -> p t (n c)"), in_=rows.rearrange("(p t) c -> p t c", t=PACK)
+                )
+                for n in range(pairs):
+                    w_raw[m, pair0 + n, g] = t[:, :, n, :]
 
-        def turn_x(i, sp, g, copy):
-            if (sp, g) == (0, 0):
-                x_grouped[i] = flow.tile([P, PASSES * NTOK * PACK], BF16, name="x_grouped", align_bytes=64)
-            words = x_raw[i, sp][:].rearrange("p s k -> p (s k)").bitcast(F32)
-            bank = psum.tile([P, 2, 2, P], F32, name="turned")
-            for s in range(2):
-                w0 = s * (D // 2) + g * (K_PASS // 2)
+        def turn_x(i, g, b0, b1):
+            bank = psum.tile([P, b1 - b0, 2, P], F32, name="turned")
+            for b in range(b0, b1):
+                words = x_raw[i, b // 2][:, b % 2, g * K_PASS : (g + 1) * K_PASS].bitcast(F32)
                 for u in range(2):
-                    nc.tensor.transpose(bank[:, s, u, :], words[:, w0 + u : w0 + K_PASS // 2 : 2], ident_f32[:])
-            o0 = g * 2 * NTOK + sp * NTOK
-            dst = x_grouped[i][:].bitcast(F32)[:, o0 : o0 + NTOK]
-            copy(out=dst.rearrange("p (s r u) -> p s r u", s=2, u=2), in_=bank[:].rearrange("p s u r -> p s r u"))
+                    nc.tensor.transpose(bank[:, b - b0, u, :], words[:, u::2], ident_f32[:])
+            if i not in x_grouped:
+                x_grouped[i] = flow.tile([P, PASSES, B, P * PACK], BF16, name="x_grouped", align_bytes=64)
+            dst = x_grouped[i][:, g, b0:b1].bitcast(F32)
+            nc.scalar.copy(out=dst.rearrange("p b (r u) -> p b r u", u=2), in_=bank[:].rearrange("p b u r -> p b r u"))
 
-        def quantize_x(i, g0, g1):
+        def quantize_x(i, g):
             nc.vector.quantize_mx(
-                out=x_codes[:, i, g0:g1, :].rearrange("p g n -> p (g n)").bitcast(FP8X4),
-                scales=x_scales[:, i, g0:g1, :].rearrange("p g n -> p (g n)"),
-                in_=x_grouped[i][:, g0 * NTOK * PACK : g1 * NTOK * PACK],
+                out=x_codes[:, i, g, :].bitcast(FP8X4),
+                scales=x_scales[:, i, g, :],
+                in_=x_grouped[i][:, g].rearrange("p b n -> p (b n)"),
             )
 
         def group_w(m, pair, g, copy):
             if g == 0:
-                w_grouped[m, pair] = flow.tile([P, PASSES, 2, P, PACK], BF16, name="w_grouped", bufs=4, align_bytes=64)
-            c0 = (pair % 2) * PAIR
-            src = w_raw[m, pair // 2, g][:, :, c0 : c0 + PAIR]
-            copy(out=w_grouped[m, pair][:, g], in_=src.rearrange("p t (m e) -> p e m t", e=2))
+                w_grouped[m, pair] = flow.tile([P, PASSES, 2, P, PACK], BF16, name="w_grouped", bufs=3, align_bytes=64)
+            copy(
+                out=w_grouped[m, pair][:, g].rearrange("p e (c n) t -> p c t n e", n=2),
+                in_=w_raw[m, pair, g].rearrange("p t (c n e) -> p c t n e", n=2, e=2),
+            )
 
-        def quantize_w(m, pair):
-            codes = flow.tile([P, PASSES, 2, P], U32, name="w_codes", bufs=6, align_bytes=64)
-            scales = flow.tile([P, PASSES, 2, P], U8, name="w_scales", bufs=6, align_bytes=64)
+        def quantize_w(m, pair, g0, g1):
+            if g0 == 0:
+                w_codes[m, pair] = flow.tile([P, PASSES, 2, P], U32, name="w_codes", bufs=8, align_bytes=64)
+                w_scales[m, pair] = flow.tile([P, PASSES, 2, P], U8, name="w_scales", bufs=8, align_bytes=64)
             nc.vector.quantize_mx(
-                out=codes[:].rearrange("p g e m -> p (g e m)").bitcast(FP8X4),
-                scales=scales[:].rearrange("p g e m -> p (g e m)"),
-                in_=w_grouped[m, pair][:].rearrange("p g e m t -> p (g e m t)"),
+                out=w_codes[m, pair][:, g0:g1].rearrange("p g e m -> p (g e m)").bitcast(FP8X4),
+                scales=w_scales[m, pair][:, g0:g1].rearrange("p g e m -> p (g e m)"),
+                in_=w_grouped[m, pair][:, g0:g1].rearrange("p g e m t -> p (g e m t)"),
             )
-            w_codes[m, pair], w_scales[m, pair] = codes, scales
 
-        def spread_tables(i0, i1):
-            n = i1 - i0
-            cos_e = cos_raw[:, i0:i1, :].rearrange("p i (j e) -> p i e j", e=2)
-            sin_e = sin_raw[:, i0:i1, :].rearrange("p i (j e) -> p i e j", e=2)
+        def spread_tables():
+            cos_e = cos_raw[:].rearrange("p i (j e) -> p i e j", e=2)
+            sin_e = sin_raw[:].rearrange("p i (j e) -> p i e j", e=2)
+            both_heads = [P, GROUPS, 2, HALF_DH]
             nc.vector.tensor_copy(
-                out=tab_rows[:, i0:i1, 0], in_=cos_e.unsqueeze(3).to_broadcast([P, n, 2, 2, 64])
+                out=table_rows[:, :, 0], in_=cos_e.unsqueeze(3).to_broadcast([P, GROUPS, 2, 2, HALF_DH])
             )
-            nc.vector.tensor_copy(
-                out=tab_rows[:, i0:i1, 1, 0], in_=sin_e[:, :, 1:2, :].to_broadcast([P, n, 2, 64])
-            )
+            nc.vector.tensor_copy(out=table_rows[:, :, 1, 0], in_=sin_e[:, :, 1:2, :].to_broadcast(both_heads))
             nc.vector.tensor_scalar(
-                out=tab_rows[:, i0:i1, 1, 1],
-                in0=sin_e[:, :, 0:1, :].to_broadcast([P, n, 2, 64]),
+                out=table_rows[:, :, 1, 1],
+                in0=sin_e[:, :, 0:1, :].to_broadcast(both_heads),
                 scalar1=-1.0,
                 scalar2=None,
                 op0=ALU.mult,
@@ -131,29 +148,23 @@ def tile_dualmultiheadattention_pa_kernel(
             bank = psum.tile([P, 2, 2, P], BF16, name="turned")
             for cs in range(2):
                 for e in range(2):
-                    src = tab_rows[:, i, cs, e].rearrange("p h j -> p (h j)")
+                    src = table_rows[:, i, cs, e].rearrange("p h j -> p (h j)")
                     nc.tensor.transpose(bank[:, cs, e, :], src, ident_bf16[:])
-            nc.scalar.copy(out=tabs[:, i], in_=bank[:])
+            nc.scalar.copy(out=tables[:, i], in_=bank[:])
 
         def turn_bias():
             bank = psum.tile([P, 2, P], BF16, name="turned")
             for e in range(2):
                 nc.tensor.transpose(bank[:, e, :], bias_rows[:, e:PAIR:2], ident_bf16[:])
-            nc.scalar.copy(out=bias_cols[:], in_=bank[:, :, 0:16])
+            nc.scalar.copy(out=bias_cols[:], in_=bank[:, :, 0 : len(weights) * PAIRS])
 
-        def unit(u):
-            r, v = divmod(u, UNITS_PER_ROUND)
-            i, pp = divmod(v, 2)
-            qk = r // 2
-            return qk, 2 * qk + (1 if i == GROUPS - 1 else 0), 2 * (r % 2) + pp, i
-
-        def multiply(u):
-            qk, m, pair, i = unit(u)
+        def multiply(n):
+            m, pair, i = units[n]
             for e in range(2):
-                bank = psum.tile([P, B, P], F32, name="acc")
+                bank = psum.tile([P, B, P], F32, name="sums")
                 for g in range(PASSES):
                     nc.tensor.matmul_mx(
-                        out=bank[:].rearrange("p b n -> p (b n)"),
+                        out=bank[:].rearrange("p b r -> p (b r)"),
                         lhsT=w_codes[m, pair][:, g, e, :].bitcast(FP8X4),
                         lhsT_scale=w_scales[m, pair][:, g, e, :],
                         rhs=x_codes[:, i, g, :].bitcast(FP8X4),
@@ -161,169 +172,166 @@ def tile_dualmultiheadattention_pa_kernel(
                         start=(g == 0),
                         stop=(g == PASSES - 1),
                     )
-                acc[u, e] = bank
+                sums[n, e] = bank
 
-        def rotate(u, e):
-            qk, m, pair, i = unit(u)
-            if e == 0:
-                prods[u] = flow.tile([P, 2, 2, B, P], F32, name="prods", bufs=4)
-            col = 4 * m + pair
-            for cs in range(2):
+        def rotate(n, e, b0, b1):
+            m, pair, i = units[n]
+            if n not in products:
+                products[n] = flow.tile([P, 2, 2, B, P], F32, name="products", bufs=3)
+            col = PAIRS * m + pair
+            for e_out in range(2):
+                cs = 0 if e_out == e else 1
                 nc.vector.scalar_tensor_tensor(
-                    out=prods[u][:, cs, e if cs == 0 else 1 - e],
-                    in0=acc[u, e][:],
+                    out=products[n][:, cs, e_out, b0:b1],
+                    in0=sums[n, e][:, b0:b1],
                     scalar=bias_cols[:, e, col : col + 1],
-                    in1=tabs[:, i, cs, e, :].unsqueeze(1).to_broadcast([P, B, P]),
+                    in1=tables[:, i, cs, e, :].unsqueeze(1).to_broadcast([P, b1 - b0, P]),
                     op0=ALU.add,
                     op1=ALU.mult,
                 )
 
-        def add_products(u):
-            sums[u] = flow.tile([P, 2, B, P], F32, name="sums")
+        def add_even(n):
+            even_added[n] = flow.tile([P, B, P], F32, name="even_added", bufs=3)
             nc.gpsimd.tensor_tensor(
-                out=sums[u][:].rearrange("p e b n -> p (e b n)"),
-                in0=prods[u][:, 0].rearrange("p e b n -> p (e b n)"),
-                in1=prods[u][:, 1].rearrange("p e b n -> p (e b n)"),
-                op=ALU.add,
+                out=even_added[n][:], in0=products[n][:, 0, 0], in1=products[n][:, 1, 0], op=ALU.add
             )
 
-        def turn_out(u):
-            qk, m, pair, i = unit(u)
-            if i == 0:
-                stage[m, pair] = flow.tile([P, 2, B, 3, DH], F32, name="stage1", bufs=3)
-            if i == GROUPS - 1:
-                stage[m, pair] = flow.tile([P, 2, B, 1, DH], F32, name="stage2")
-            for hb in range(2):
-                bank = psum.tile([P, 2, 2, 2, 64], F32, name="turned")
-                for s in range(2):
-                    b = 2 * hb + s
-                    for e in range(2):
-                        dst = bank[:, s, :, e, :]
-                        if u % 2 == 0:
-                            nc.tensor.transpose(dst, sums[u][:, e, b, :], ident_f32[:])
-                        else:
-                            for cs in range(2):
-                                nc.tensor.matmul(
-                                    dst,
-                                    lhsT=prods[u][:, cs, e, b, :],
-                                    rhs=ident_f32[:],
-                                    start=(cs == 0),
-                                    stop=(cs == 1),
-                                    is_transpose=True,
-                                )
-                dst = stage[m, pair][:, :, 2 * hb : 2 * hb + 2, i % 3, :].rearrange("p h s (j e) -> p s h j e", e=2)
-                src = bank[:].rearrange("p s h e j -> p s h j e")
-                if qk == 0:
-                    nc.scalar.activation(out=dst, in_=src, func=ACT.Copy, scale=Q_SCALE)
-                else:
-                    nc.scalar.copy(out=dst, in_=src)
-
-        def store(u):
-            qk, m, pair, i = unit(u)
-            last_round = u >= UNITS - UNITS_PER_ROUND
-            if i == 3:
-                i0, i1 = 0, 1
-            elif i == 2:
-                i0, i1 = (2, 3) if last_round else (0, 3)
-            elif i == 1 and last_round:
-                i0, i1 = 0, 2
-            else:
-                return
-            for hh in range(2):
-                head = outs[qk][:, 2 * pair + hh]
-                if i == 3:
-                    rows = head[:, N1:, :].rearrange("b (p i) c -> p b i c", i=1)
-                else:
-                    rows = head[:, :N1, :].rearrange("b (p i) c -> p b i c", i=3)
-                nc.sync.dma_start(
-                    out=rows[:, :, i0:i1, :].rearrange("p b i c -> p b (i c)"),
-                    in_=stage[m, pair][:, hh, :, i0:i1, :].rearrange("p b i c -> p b (i c)"),
+        def turn_out(n, b, e, terms):
+            if (n, b // 2) not in turned:
+                turned[n, b // 2] = psum.tile([P, 2, 2, P], F32, name="turned")
+            for k, term in enumerate(terms):
+                nc.tensor.matmul(
+                    turned[n, b // 2][:, b % 2, e, :],
+                    lhsT=term,
+                    rhs=ident_f32[:],
+                    start=(k == 0),
+                    stop=(k == len(terms) - 1),
+                    is_transpose=True,
                 )
 
-        v_copy, s_copy = nc.vector.tensor_copy, nc.scalar.copy
+        def copy_out(n, hb):
+            m, pair, i = units[n]
+            if (m, pair) not in staged:
+                if i < GROUPS1:
+                    staged[m, pair] = flow.tile([P, B, 2, GROUPS1, DH], F32, name="staged1", bufs=5)
+                else:
+                    staged[m, pair] = flow.tile([P, B, 2, 1, DH], F32, name="staged2", bufs=4)
+            dst = staged[m, pair][:, 2 * hb : 2 * hb + 2, :, i % GROUPS1, :].rearrange("p b h (j e) -> p b h j e", e=2)
+            src = turned[n, hb][:].rearrange("p b e (h j) -> p b h j e", h=2)
+            if m in (WQ1, WQ2):
+                nc.scalar.activation(out=dst, in_=src, func=ACT.Copy, scale=Q_SCALE)
+            else:
+                nc.scalar.copy(out=dst, in_=src)
 
-        load_x(0)
-        load_w(0, 0)
-        load_x(1)
-        load_w(1, 0)
-        load_x(2)
-        load_x(3)
-        load_w(0, 1)
-        load_w(1, 1)
+        def store(n, b0, b1):
+            m, pair, i = units[n]
+            for h in range(2):
+                head = outs[m][b0:b1, 2 * pair + h]
+                if i < GROUPS1:
+                    rows = head[:, :N1, :].rearrange("b (p i) c -> p b (i c)", i=GROUPS1)
+                else:
+                    rows = head[:, N1:, :].rearrange("b p c -> p b c")
+                nc.sync.dma_start(out=rows, in_=staged[m, pair][:, b0:b1, h].rearrange("p b i c -> p b (i c)"))
+
+        nc.sync.dma_start(out=cos_raw[:, :GROUPS1, :], in_=cos1.rearrange("(p i) c -> p i c", i=GROUPS1))
+        nc.sync.dma_start(out=sin_raw[:, :GROUPS1, :], in_=sin1.rearrange("(p i) c -> p i c", i=GROUPS1))
+        nc.sync.dma_start(out=cos_raw[:, GROUPS1, :], in_=cos2)
+        nc.sync.dma_start(out=sin_raw[:, GROUPS1, :], in_=sin2)
+        load_x(0, 0)
+        load_x(0, 1)
+        for pair in range(PAIRS - 1):
+            load_w(WQ1, pair, 1, "raw_wq1")
+        load_x(1, 0)
+        load_w(WQ1, PAIRS - 1, 1, "raw_wq1")
+        load_x(1, 1)
+        load_x(2, 0)
+        load_x(2, 1)
+        load_w(*later_pairs[0], 2, "raw")
         nc.vector.memset(bias_rows[:], 0.0)
         make_identity(nc, ident_f32[:])
-        nc.gpsimd.dma_start(out=cos_raw[:, 0:3, :], in_=cos1.rearrange("(p i) c -> p i c", i=3))
-        nc.gpsimd.dma_start(out=sin_raw[:, 0:3, :], in_=sin1.rearrange("(p i) c -> p i c", i=3))
-        for m in range(4):
-            nc.gpsimd.dma_start(out=bias_rows[4 * m : 4 * m + 4, :], in_=biases[m].rearrange("(r c) -> r c", c=PAIR))
-        nc.gpsimd.dma_start(out=cos_raw[:, 3, :], in_=cos2)
-        nc.gpsimd.dma_start(out=sin_raw[:, 3, :], in_=sin2)
+        for m in range(len(weights)):
+            rows = bias_rows[PAIRS * m : PAIRS * (m + 1), :]
+            nc.gpsimd.dma_start(out=rows, in_=biases[m].rearrange("(r c) -> r c", c=PAIR))
         nc.vector.tensor_copy(out=ident_bf16[:], in_=ident_f32[:])
 
-        turn_x(0, 0, 0, v_copy)
-        turn_x(0, 0, 1, s_copy)
-        spread_tables(0, 1)
-        turn_x(0, 1, 0, s_copy)
-        group_w(0, 0, 0, v_copy)
-        turn_x(0, 1, 1, s_copy)
-        group_w(0, 0, 1, v_copy)
-        turn_tables(0)
+        spread_tables()
+        for hb in range(2):
+            for g in range(PASSES):
+                turn_x(0, g, 2 * hb, 2 * hb + 2)
+        for g in range(PASSES):
+            group_w(WQ1, 0, g, nc.vector.tensor_copy)
+        quantize_x(0, 0)
+        quantize_w(WQ1, 0, 0, PASSES)
+        quantize_x(0, 1)
         turn_bias()
-        quantize_x(0, 0, 1)
-        quantize_w(0, 0)
-        quantize_x(0, 1, 2)
-        group_w(0, 1, 0, s_copy)
-        group_w(0, 1, 1, v_copy)
-        turn_x(1, 0, 0, s_copy)
-        turn_x(1, 0, 1, s_copy)
+        turn_tables(0)
+        turn_tables(1)
         multiply(0)
-        quantize_w(0, 1)
+        for g in range(PASSES):
+            group_w(WQ1, 1, g, nc.vector.tensor_copy)
+        for g in range(PASSES):
+            group_w(WQ1, 2, g, nc.scalar.copy)
+        quantize_w(WQ1, 1, 0, PASSES)
+        for g in range(PASSES):
+            group_w(WQ1, 3, g, nc.scalar.copy)
+        for g in range(PASSES):
+            turn_x(1, g, 0, 2)
 
-        later = []
-        for r in range(ROUNDS):
-            for v in (6, 7, 8, 9):
-                if r * UNITS_PER_ROUND + v < UNITS:
-                    later.append(unit(r * UNITS_PER_ROUND + v)[1:3])
-        pieces = [(m, pair, g) for (m, pair) in later for g in range(PASSES)]
-        pieces_done, pairs_done = 0, 0
+        x_turns = {0: [(1, g, 2, B) for g in range(PASSES)]}
+        x_quantize = {1 + g: (1, g) for g in range(PASSES)}
+        for i, slot0, batches in ((2, X2_SLOT, 2), (3, X3_SLOT, 1)):
+            steps = B // batches
+            for g in range(PASSES):
+                for s in range(steps):
+                    x_turns[slot0 + steps * g + s] = [(i, g, batches * s, batches * (s + 1))]
+                x_quantize[slot0 + steps * (g + 1) - 1 + QUANTIZE_X_LAG] = (i, g)
+        table_turns = {[i for m, pair, i in units].index(i) - TABLE_LEAD: i for i in range(2, GROUPS)}
+        w_loads = {2 * n: later_pairs[n + 2] for n in range(0, len(later_pairs) - 2, 2)}
 
-        for u in range(UNITS + 2):
-            if u == 0:
-                turn_x(1, 1, 0, s_copy)
-                turn_x(1, 1, 1, s_copy)
-            if u + 1 < UNITS:
-                multiply(u + 1)
-            if u == 4:
-                load_w(2, 0)
-                load_w(3, 0)
-            if u == 12:
-                load_w(2, 1)
-                load_w(3, 1)
-            if u >= 1 and (u - 1) % 2 == 0 and u - 1 < UNITS:
-                add_products(u - 1)
-            if u < UNITS:
-                rotate(u, 0)
-                if u in (2, 4):
-                    quantize_x(u // 2 + 1, 0, PASSES)
-                for n in range({2: 1, 4: 1, 6: 2}.get(u % UNITS_PER_ROUND, 0)):
-                    if pairs_done < len(later):
-                        quantize_w(*later[pairs_done])
-                        pairs_done += 1
-                rotate(u, 1)
-            if u == 0:
-                quantize_x(1, 0, PASSES)
-                spread_tables(1, GROUPS)
-            if u >= 2:
-                turn_out(u - 2)
-                store(u - 2)
-            if u == 1:
-                for i in range(1, GROUPS):
-                    turn_tables(i)
-            if u in (1, 3):
-                for sp in range(2):
-                    for g in range(PASSES):
-                        turn_x((u + 3) // 2, sp, g, s_copy)
-            for n in range(2 if u in (2, 4) else 1):
-                if pieces_done < len(pieces):
-                    group_w(*pieces[pieces_done], s_copy)
-                    pieces_done += 1
+        for n in range(last + 1):
+            if n < last:
+                multiply(n + 1)
+            for job in x_turns.get(n, []):
+                turn_x(*job)
+            if n in table_turns:
+                turn_tables(table_turns[n])
+            if n > 0:
+                done = n - 1
+                for hb in range(2):
+                    for b in (2 * hb, 2 * hb + 1):
+                        turn_out(done, b, 1, [products[done][:, cs, 1, b, :] for cs in range(2)])
+                    for b in (2 * hb, 2 * hb + 1):
+                        turn_out(done, b, 0, [even_added[done][:, b, :]])
+                    copy_out(done, hb)
+                if units[done][2] >= GROUPS1 - 1:
+                    store(done, 0, B)
+            if 0 <= n - GROUP_W_SLOT < len(later_passes):
+                group_w(*later_passes[n - GROUP_W_SLOT], nc.scalar.copy)
+            if n in w_loads:
+                load_w(*w_loads[n], 2, "raw")
+            if n == 0:
+                load_x(GROUPS1, 0)
+                load_x(GROUPS1, 1)
+            if n < last:
+                rotate(n, 0, 0, B)
+                if n + 2 < PAIRS:
+                    quantize_w(WQ1, n + 2, 0, PASSES)
+                if n in x_quantize:
+                    quantize_x(*x_quantize[n])
+                if 0 <= n - GROUP_W_SLOT - QUANTIZE_W_LAG < len(later_passes):
+                    m, pair, g = later_passes[n - GROUP_W_SLOT - QUANTIZE_W_LAG]
+                    quantize_w(m, pair, g, g + 1)
+                rotate(n, 1, 0, B)
+                add_even(n)
+
+        for hb in range(2):
+            b0, b1 = 2 * hb, 2 * hb + 2
+            rotate(last, 0, b0, b1)
+            rotate(last, 1, b0, b1)
+            both = products[last][:, 0, :, b0:b1]
+            nc.vector.tensor_tensor(out=both, in0=both, in1=products[last][:, 1, :, b0:b1], op=ALU.add)
+            for b in range(b0, b1):
+                for e in range(2):
+                    turn_out(last, b, e, [products[last][:, 0, e, b, :]])
+            copy_out(last, hb)
+            store(last, b0, b1)

@@ -33,6 +33,7 @@ QUANTIZE_W_LAG = 2
 X2_SLOT = 1
 X3_SLOT = 7
 QUANTIZE_X_LAG = 2
+GPSIMD_PLACES = 6
 TABLE_LEAD = 2
 
 
@@ -47,9 +48,9 @@ def tile_dualmultiheadattention_pa_kernel(
     x_rows = [x1_rows[i] for i in range(GROUPS1)] + [x_2.rearrange("b p k -> p b k")]
 
     units = [(WQ1, pair, i) for i in range(GROUPS1) for pair in range(PAIRS)]
-    for half, weight2 in enumerate((WQ2, WK2)):
-        units += [(WK1, 2 * half + n, i) for n in range(2) for i in range(GROUPS1)]
-        units += [(weight2, pair, GROUPS1) for pair in range(PAIRS)]
+    units2 = [(m, pair, GROUPS1) for m in (WQ2, WK2) for pair in range(PAIRS)]
+    units += [(WK1, pair, i) for pair in (0, 1) for i in range(GROUPS1)] + units2[:2]
+    units += [(WK1, pair, i) for pair in (2, 3) for i in range(GROUPS1)] + units2[2:]
     last = len(units) - 1
     later_pairs = []
     for m, pair, i in units:
@@ -70,12 +71,12 @@ def tile_dualmultiheadattention_pa_kernel(
         bias_rows = keep.tile([P, PAIR], BF16)
         bias_cols = keep.tile([P, 2, len(weights) * PAIRS], F32)
         table_rows = keep.tile([P, GROUPS, 2, 2, 2, HALF_DH], BF16)
-        tables = keep.tile([P, GROUPS, 2, 2, P], BF16)
+        tables = keep.tile([P, GROUPS, 2, 2, B, P], BF16)
         x_codes = keep.tile([P, GROUPS, PASSES, NTOK], U32, align_bytes=64)
         x_scales = keep.tile([P, GROUPS, PASSES, NTOK], U8, align_bytes=64)
 
         x_raw, x_grouped, w_raw, w_grouped, w_codes, w_scales = {}, {}, {}, {}, {}, {}
-        sums, products, even_added, turned, staged = {}, {}, {}, {}, {}
+        sums, products, added, turned, staged = {}, {}, {}, {}, {}
 
         def load_x(i, hb):
             t = flow.tile([P, 2, D], BF16, name="raw", bufs=8)
@@ -120,8 +121,8 @@ def tile_dualmultiheadattention_pa_kernel(
 
         def quantize_w(m, pair, g0, g1):
             if g0 == 0:
-                w_codes[m, pair] = flow.tile([P, PASSES, 2, P], U32, name="w_codes", bufs=8, align_bytes=64)
-                w_scales[m, pair] = flow.tile([P, PASSES, 2, P], U8, name="w_scales", bufs=8, align_bytes=64)
+                w_codes[m, pair] = flow.tile([P, PASSES, 2, P], U32, name="w_codes", bufs=6, align_bytes=64)
+                w_scales[m, pair] = flow.tile([P, PASSES, 2, P], U8, name="w_scales", bufs=6, align_bytes=64)
             nc.vector.quantize_mx(
                 out=w_codes[m, pair][:, g0:g1].rearrange("p g e m -> p (g e m)").bitcast(FP8X4),
                 scales=w_scales[m, pair][:, g0:g1].rearrange("p g e m -> p (g e m)"),
@@ -146,11 +147,11 @@ def tile_dualmultiheadattention_pa_kernel(
 
         def turn_tables(i):
             bank = psum.tile([P, 2, 2, P], BF16, name="turned")
-            for cs in range(2):
-                for e in range(2):
-                    src = table_rows[:, i, cs, e].rearrange("p h j -> p (h j)")
-                    nc.tensor.transpose(bank[:, cs, e, :], src, ident_bf16[:])
-            nc.scalar.copy(out=tables[:, i], in_=bank[:])
+            for e in range(2):
+                for e_out in range(2):
+                    src = table_rows[:, i, 0 if e_out == e else 1, e].rearrange("p h j -> p (h j)")
+                    nc.tensor.transpose(bank[:, e, e_out, :], src, ident_bf16[:])
+            nc.scalar.copy(out=tables[:, i], in_=bank[:].unsqueeze(3).to_broadcast([P, 2, 2, B, P]))
 
         def turn_bias():
             bank = psum.tile([P, 2, P], BF16, name="turned")
@@ -176,36 +177,37 @@ def tile_dualmultiheadattention_pa_kernel(
 
         def rotate(n, e, b0, b1):
             m, pair, i = units[n]
-            if n not in products:
-                products[n] = flow.tile([P, 2, 2, B, P], F32, name="products", bufs=3)
+            if e == 0:
+                products[n, b0] = flow.tile([P, 2, 2, b1 - b0, P], F32, name="products", bufs=3)
             col = PAIRS * m + pair
-            for e_out in range(2):
-                cs = 0 if e_out == e else 1
-                nc.vector.scalar_tensor_tensor(
-                    out=products[n][:, cs, e_out, b0:b1],
-                    in0=sums[n, e][:, b0:b1],
-                    scalar=bias_cols[:, e, col : col + 1],
-                    in1=tables[:, i, cs, e, :].unsqueeze(1).to_broadcast([P, b1 - b0, P]),
-                    op0=ALU.add,
-                    op1=ALU.mult,
-                )
-
-        def add_even(n):
-            even_added[n] = flow.tile([P, B, P], F32, name="even_added", bufs=3)
-            nc.gpsimd.tensor_tensor(
-                out=even_added[n][:], in0=products[n][:, 0, 0], in1=products[n][:, 1, 0], op=ALU.add
+            width = (b1 - b0) * P
+            nc.vector.scalar_tensor_tensor(
+                out=products[n, b0][:, e].rearrange("p o b r -> p o (b r)"),
+                in0=sums[n, e][:, b0:b1].rearrange("p b r -> p (b r)").unsqueeze(1).to_broadcast([P, 2, width]),
+                scalar=bias_cols[:, e, col : col + 1],
+                in1=tables[:, i, e, :, b0:b1].rearrange("p o b r -> p o (b r)"),
+                op0=ALU.add,
+                op1=ALU.mult,
             )
 
-        def turn_out(n, b, e, terms):
+        def add_terms(n):
+            added[n] = flow.tile([P, GPSIMD_PLACES, P], F32, name="added", bufs=3)
+            places = products[n, 0][:].rearrange("p e o b r -> p e (o b) r")[:, :, :GPSIMD_PLACES]
+            nc.gpsimd.tensor_tensor(out=added[n][:], in0=places[:, 0], in1=places[:, 1], op=ALU.add)
+
+        def terms(n, b0, b, e_out):
+            return [products[n, b0][:, e, e_out, b - b0, :] for e in range(2)]
+
+        def turn_out(n, b, e, parts):
             if (n, b // 2) not in turned:
                 turned[n, b // 2] = psum.tile([P, 2, 2, P], F32, name="turned")
-            for k, term in enumerate(terms):
+            for k, part in enumerate(parts):
                 nc.tensor.matmul(
                     turned[n, b // 2][:, b % 2, e, :],
-                    lhsT=term,
+                    lhsT=part,
                     rhs=ident_f32[:],
                     start=(k == 0),
-                    stop=(k == len(terms) - 1),
+                    stop=(k == len(parts) - 1),
                     is_transpose=True,
                 )
 
@@ -215,7 +217,7 @@ def tile_dualmultiheadattention_pa_kernel(
                 if i < GROUPS1:
                     staged[m, pair] = flow.tile([P, B, 2, GROUPS1, DH], F32, name="staged1", bufs=5)
                 else:
-                    staged[m, pair] = flow.tile([P, B, 2, 1, DH], F32, name="staged2", bufs=4)
+                    staged[m, pair] = flow.tile([P, B, 2, 1, DH], F32, name="staged2", bufs=3)
             dst = staged[m, pair][:, 2 * hb : 2 * hb + 2, :, i % GROUPS1, :].rearrange("p b h (j e) -> p b h j e", e=2)
             src = turned[n, hb][:].rearrange("p b e (h j) -> p b h j e", h=2)
             if m in (WQ1, WQ2):
@@ -239,7 +241,12 @@ def tile_dualmultiheadattention_pa_kernel(
         nc.sync.dma_start(out=sin_raw[:, GROUPS1, :], in_=sin2)
         load_x(0, 0)
         load_x(0, 1)
-        for pair in range(PAIRS - 1):
+        load_w(WQ1, 0, 1, "raw_wq1")
+        nc.vector.memset(bias_rows[:], 0.0)
+        for m in range(len(weights)):
+            rows = bias_rows[PAIRS * m : PAIRS * (m + 1), :]
+            nc.sync.dma_start(out=rows, in_=biases[m].rearrange("(r c) -> r c", c=PAIR))
+        for pair in range(1, PAIRS - 1):
             load_w(WQ1, pair, 1, "raw_wq1")
         load_x(1, 0)
         load_w(WQ1, PAIRS - 1, 1, "raw_wq1")
@@ -247,11 +254,7 @@ def tile_dualmultiheadattention_pa_kernel(
         load_x(2, 0)
         load_x(2, 1)
         load_w(*later_pairs[0], 2, "raw")
-        nc.vector.memset(bias_rows[:], 0.0)
         make_identity(nc, ident_f32[:])
-        for m in range(len(weights)):
-            rows = bias_rows[PAIRS * m : PAIRS * (m + 1), :]
-            nc.gpsimd.dma_start(out=rows, in_=biases[m].rearrange("(r c) -> r c", c=PAIR))
         nc.vector.tensor_copy(out=ident_bf16[:], in_=ident_f32[:])
 
         spread_tables()
@@ -265,7 +268,6 @@ def tile_dualmultiheadattention_pa_kernel(
         quantize_x(0, 1)
         turn_bias()
         turn_tables(0)
-        turn_tables(1)
         multiply(0)
         for g in range(PASSES):
             group_w(WQ1, 1, g, nc.vector.tensor_copy)
@@ -285,7 +287,8 @@ def tile_dualmultiheadattention_pa_kernel(
                 for s in range(steps):
                     x_turns[slot0 + steps * g + s] = [(i, g, batches * s, batches * (s + 1))]
                 x_quantize[slot0 + steps * (g + 1) - 1 + QUANTIZE_X_LAG] = (i, g)
-        table_turns = {[i for m, pair, i in units].index(i) - TABLE_LEAD: i for i in range(2, GROUPS)}
+        unit_groups = [unit[2] for unit in units]
+        table_turns = {0: 1, **{unit_groups.index(i) - TABLE_LEAD: i for i in range(2, GROUPS)}}
         w_loads = {2 * n: later_pairs[n + 2] for n in range(0, len(later_pairs) - 2, 2)}
 
         for n in range(last + 1):
@@ -297,11 +300,12 @@ def tile_dualmultiheadattention_pa_kernel(
                 turn_tables(table_turns[n])
             if n > 0:
                 done = n - 1
-                for hb in range(2):
-                    for b in (2 * hb, 2 * hb + 1):
-                        turn_out(done, b, 1, [products[done][:, cs, 1, b, :] for cs in range(2)])
-                    for b in (2 * hb, 2 * hb + 1):
-                        turn_out(done, b, 0, [even_added[done][:, b, :]])
+                for s in range(GPSIMD_PLACES, 2 * B):
+                    turn_out(done, s % B, s // B, terms(done, 0, s % B, s // B))
+                for hb in (1, 0):
+                    for s in range(GPSIMD_PLACES):
+                        if s % B // 2 == hb:
+                            turn_out(done, s % B, s // B, [added[done][:, s, :]])
                     copy_out(done, hb)
                 if units[done][2] >= GROUPS1 - 1:
                     store(done, 0, B)
@@ -314,6 +318,7 @@ def tile_dualmultiheadattention_pa_kernel(
                 load_x(GROUPS1, 1)
             if n < last:
                 rotate(n, 0, 0, B)
+                rotate(n, 1, 0, B)
                 if n + 2 < PAIRS:
                     quantize_w(WQ1, n + 2, 0, PASSES)
                 if n in x_quantize:
@@ -321,17 +326,14 @@ def tile_dualmultiheadattention_pa_kernel(
                 if 0 <= n - GROUP_W_SLOT - QUANTIZE_W_LAG < len(later_passes):
                     m, pair, g = later_passes[n - GROUP_W_SLOT - QUANTIZE_W_LAG]
                     quantize_w(m, pair, g, g + 1)
-                rotate(n, 1, 0, B)
-                add_even(n)
+                add_terms(n)
 
         for hb in range(2):
             b0, b1 = 2 * hb, 2 * hb + 2
             rotate(last, 0, b0, b1)
             rotate(last, 1, b0, b1)
-            both = products[last][:, 0, :, b0:b1]
-            nc.vector.tensor_tensor(out=both, in0=both, in1=products[last][:, 1, :, b0:b1], op=ALU.add)
             for b in range(b0, b1):
                 for e in range(2):
-                    turn_out(last, b, e, [products[last][:, 0, e, b, :]])
+                    turn_out(last, b, e, terms(last, b0, b, e))
             copy_out(last, hb)
             store(last, b0, b1)

from contextlib import ExitStack

import concourse.mybir as mybir
from concourse.masks import make_identity

B, N1, N2, D, H, DH = 4, 384, 128, 1024, 8, 128
E = H * DH
FLOPS = 2 * 2 * B * (N1 + N2) * D * E

F32 = mybir.dt.float32
BF16 = mybir.dt.bfloat16
U32 = mybir.dt.uint32
U8 = mybir.dt.uint8
FP8X4 = mybir.dt.float8_e5m2_x4
ALU = mybir.AluOpType
ACT = mybir.ActivationFunctionType

P = 128
PACK = 4
K_PASS = P * PACK
PASSES = D // K_PASS
GROUPS1 = N1 // P
GROUPS = GROUPS1 + 1
NTOK = B * P
PAIR = 2 * DH
PAIRS = H // 2
HALF_DH = DH // 2
WQ1, WQ2, WK1, WK2 = range(4)
Q_SCALE = DH ** -0.5

GROUP_W_SLOT = 2
QUANTIZE_W_LAG = 2
X2_SLOT = 1
X3_SLOT = 7
QUANTIZE_X_LAG = 2
GPSIMD_PLACES = 6
TABLE_LEAD = 2


def tile_dualmultiheadattention_pa_kernel(
    tc, x_1, x_2, cos1, sin1, cos2, sin2, wq1, bq1, wk1, bk1, wq2, bq2, wk2, bk2, out_0, out_1
):
    nc = tc.nc
    weights = [wq1, wq2, wk1, wk2]
    biases = [bq1, bq2, bk1, bk2]
    outs = [out_0, out_0, out_1, out_1]
    x1_rows = x_1.rearrange("b (p i) k -> i p b k", i=GROUPS1)
    x_rows = [x1_rows[i] for i in range(GROUPS1)] + [x_2.rearrange("b p k -> p b k")]

    units = [(WQ1, pair, i) for i in range(GROUPS1) for pair in range(PAIRS)]
    units2 = [(m, pair, GROUPS1) for m in (WQ2, WK2) for pair in range(PAIRS)]
    units += [(WK1, pair, i) for pair in (0, 1) for i in range(GROUPS1)] + units2[:2]
    units += [(WK1, pair, i) for pair in (2, 3) for i in range(GROUPS1)] + units2[2:]
    last = len(units) - 1
    later_pairs = []
    for m, pair, i in units:
        if m != WQ1 and (m, pair) not in later_pairs:
            later_pairs.append((m, pair))
    later_passes = [(m, pair, g) for m, pair in later_pairs for g in range(PASSES)]

    with ExitStack() as ctx:
        keep = ctx.enter_context(tc.tile_pool(name="keep", bufs=1))
        flow = ctx.enter_context(tc.tile_pool(name="flow", bufs=2))
        psum = ctx.enter_context(tc.psum_pool(name="psum", bufs=4))
        ctx.enter_context(tc.manual_schedule())

        ident_f32 = keep.tile([P, P], F32)
        ident_bf16 = keep.tile([P, P], BF16)
        cos_raw = keep.tile([P, GROUPS, DH], BF16)
        sin_raw = keep.tile([P, GROUPS, DH], BF16)
        bias_rows = keep.tile([P, PAIR], BF16)
        bias_cols = keep.tile([P, 2, len(weights) * PAIRS], F32)
        table_rows = keep.tile([P, GROUPS, 2, 2, 2, HALF_DH], BF16)
        tables = keep.tile([P, GROUPS, 2, 2, B, P], BF16)
        x_codes = keep.tile([P, GROUPS, PASSES, NTOK], U32, align_bytes=64)
        x_scales = keep.tile([P, GROUPS, PASSES, NTOK], U8, align_bytes=64)

        x_raw, x_grouped, w_raw, w_grouped, w_codes, w_scales = {}, {}, {}, {}, {}, {}
        sums, products, added, turned, staged = {}, {}, {}, {}, {}

        def load_x(i, hb):
            t = flow.tile([P, 2, D], BF16, name="raw", bufs=8)
            nc.sync.dma_start(out=t[:], in_=x_rows[i][:, 2 * hb : 2 * hb + 2, :])
            x_raw[i, hb] = t

        def load_w(m, pair0, pairs, tag):
            for g in range(PASSES):
                t = flow.tile([P, PACK, pairs, PAIR], BF16, name=tag, bufs=8)
                rows = weights[m][g * K_PASS : (g + 1) * K_PASS, pair0 * PAIR : (pair0 + pairs) * PAIR]
                nc.sync.dma_start(
                    out=t[:].rearrange("p t n c -> p t (n c)"), in_=rows.rearrange("(p t) c -> p t c", t=PACK)
                )
                for n in range(pairs):
                    w_raw[m, pair0 + n, g] = t[:, :, n, :]

        def turn_x(i, g, b0, b1):
            bank = psum.tile([P, b1 - b0, 2, P], F32, name="turned")
            for b in range(b0, b1):
                words = x_raw[i, b // 2][:, b % 2, g * K_PASS : (g + 1) * K_PASS].bitcast(F32)
                for u in range(2):
                    nc.tensor.transpose(bank[:, b - b0, u, :], words[:, u::2], ident_f32[:])
            if i not in x_grouped:
                x_grouped[i] = flow.tile([P, PASSES, B, P * PACK], BF16, name="x_grouped", align_bytes=64)
            dst = x_grouped[i][:, g, b0:b1].bitcast(F32)
            nc.scalar.copy(out=dst.rearrange("p b (r u) -> p b r u", u=2), in_=bank[:].rearrange("p b u r -> p b r u"))

        def quantize_x(i, g):
            nc.vector.quantize_mx(
                out=x_codes[:, i, g, :].bitcast(FP8X4),
                scales=x_scales[:, i, g, :],
                in_=x_grouped[i][:, g].rearrange("p b n -> p (b n)"),
            )

        def group_w(m, pair, g, copy):
            if g == 0:
                w_grouped[m, pair] = flow.tile([P, PASSES, 2, P, PACK], BF16, name="w_grouped", bufs=3, align_bytes=64)
            copy(
                out=w_grouped[m, pair][:, g].rearrange("p e (c n) t -> p c t n e", n=2),
                in_=w_raw[m, pair, g].rearrange("p t (c n e) -> p c t n e", n=2, e=2),
            )

        def quantize_w(m, pair, g0, g1):
            if g0 == 0:
                w_codes[m, pair] = flow.tile([P, PASSES, 2, P], U32, name="w_codes", bufs=6, align_bytes=64)
                w_scales[m, pair] = flow.tile([P, PASSES, 2, P], U8, name="w_scales", bufs=6, align_bytes=64)
            nc.vector.quantize_mx(
                out=w_codes[m, pair][:, g0:g1].rearrange("p g e m -> p (g e m)").bitcast(FP8X4),
                scales=w_scales[m, pair][:, g0:g1].rearrange("p g e m -> p (g e m)"),
                in_=w_grouped[m, pair][:, g0:g1].rearrange("p g e m t -> p (g e m t)"),
            )

        def spread_tables():
            cos_e = cos_raw[:].rearrange("p i (j e) -> p i e j", e=2)
            sin_e = sin_raw[:].rearrange("p i (j e) -> p i e j", e=2)
            both_heads = [P, GROUPS, 2, HALF_DH]
            nc.vector.tensor_copy(
                out=table_rows[:, :, 0], in_=cos_e.unsqueeze(3).to_broadcast([P, GROUPS, 2, 2, HALF_DH])
            )
            nc.vector.tensor_copy(out=table_rows[:, :, 1, 0], in_=sin_e[:, :, 1:2, :].to_broadcast(both_heads))
            nc.vector.tensor_scalar(
                out=table_rows[:, :, 1, 1],
                in0=sin_e[:, :, 0:1, :].to_broadcast(both_heads),
                scalar1=-1.0,
                scalar2=None,
                op0=ALU.mult,
            )

        def turn_tables(i):
            bank = psum.tile([P, 2, 2, P], BF16, name="turned")
            for e in range(2):
                for e_out in range(2):
                    src = table_rows[:, i, 0 if e_out == e else 1, e].rearrange("p h j -> p (h j)")
                    nc.tensor.transpose(bank[:, e, e_out, :], src, ident_bf16[:])
            nc.scalar.copy(out=tables[:, i], in_=bank[:].unsqueeze(3).to_broadcast([P, 2, 2, B, P]))

        def turn_bias():
            bank = psum.tile([P, 2, P], BF16, name="turned")
            for e in range(2):
                nc.tensor.transpose(bank[:, e, :], bias_rows[:, e:PAIR:2], ident_bf16[:])
            nc.scalar.copy(out=bias_cols[:], in_=bank[:, :, 0 : len(weights) * PAIRS])

        def multiply(n):
            m, pair, i = units[n]
            for e in range(2):
                bank = psum.tile([P, B, P], F32, name="sums")
                for g in range(PASSES):
                    nc.tensor.matmul_mx(
                        out=bank[:].rearrange("p b r -> p (b r)"),
                        lhsT=w_codes[m, pair][:, g, e, :].bitcast(FP8X4),
                        lhsT_scale=w_scales[m, pair][:, g, e, :],
                        rhs=x_codes[:, i, g, :].bitcast(FP8X4),
                        rhs_scale=x_scales[:, i, g, :],
                        start=(g == 0),
                        stop=(g == PASSES - 1),
                    )
                sums[n, e] = bank

        def rotate(n, e, b0, b1):
            m, pair, i = units[n]
            if e == 0:
                products[n, b0] = flow.tile([P, 2, 2, b1 - b0, P], F32, name="products", bufs=3)
            col = PAIRS * m + pair
            width = (b1 - b0) * P
            nc.vector.scalar_tensor_tensor(
                out=products[n, b0][:, e].rearrange("p o b r -> p o (b r)"),
                in0=sums[n, e][:, b0:b1].rearrange("p b r -> p (b r)").unsqueeze(1).to_broadcast([P, 2, width]),
                scalar=bias_cols[:, e, col : col + 1],
                in1=tables[:, i, e, :, b0:b1].rearrange("p o b r -> p o (b r)"),
                op0=ALU.add,
                op1=ALU.mult,
            )

        def add_terms(n):
            added[n] = flow.tile([P, GPSIMD_PLACES, P], F32, name="added", bufs=3)
            places = products[n, 0][:].rearrange("p e o b r -> p e (o b) r")[:, :, :GPSIMD_PLACES]
            nc.gpsimd.tensor_tensor(out=added[n][:], in0=places[:, 0], in1=places[:, 1], op=ALU.add)

        def terms(n, b0, b, e_out):
            return [products[n, b0][:, e, e_out, b - b0, :] for e in range(2)]

        def turn_out(n, b, e, parts):
            if (n, b // 2) not in turned:
                turned[n, b // 2] = psum.tile([P, 2, 2, P], F32, name="turned")
            for k, part in enumerate(parts):
                nc.tensor.matmul(
                    turned[n, b // 2][:, b % 2, e, :],
                    lhsT=part,
                    rhs=ident_f32[:],
                    start=(k == 0),
                    stop=(k == len(parts) - 1),
                    is_transpose=True,
                )

        def copy_out(n, hb):
            m, pair, i = units[n]
            if (m, pair) not in staged:
                if i < GROUPS1:
                    staged[m, pair] = flow.tile([P, B, 2, GROUPS1, DH], F32, name="staged1", bufs=5)
                else:
                    staged[m, pair] = flow.tile([P, B, 2, 1, DH], F32, name="staged2", bufs=3)
            dst = staged[m, pair][:, 2 * hb : 2 * hb + 2, :, i % GROUPS1, :].rearrange("p b h (j e) -> p b h j e", e=2)
            src = turned[n, hb][:].rearrange("p b e (h j) -> p b h j e", h=2)
            if m in (WQ1, WQ2):
                nc.scalar.activation(out=dst, in_=src, func=ACT.Copy, scale=Q_SCALE)
            else:
                nc.scalar.copy(out=dst, in_=src)

        def store(n, b0, b1):
            m, pair, i = units[n]
            for h in range(2):
                head = outs[m][b0:b1, 2 * pair + h]
                if i < GROUPS1:
                    rows = head[:, :N1, :].rearrange("b (p i) c -> p b (i c)", i=GROUPS1)
                else:
                    rows = head[:, N1:, :].rearrange("b p c -> p b c")
                nc.sync.dma_start(out=rows, in_=staged[m, pair][:, b0:b1, h].rearrange("p b i c -> p b (i c)"))

        nc.sync.dma_start(out=cos_raw[:, :GROUPS1, :], in_=cos1.rearrange("(p i) c -> p i c", i=GROUPS1))
        nc.sync.dma_start(out=sin_raw[:, :GROUPS1, :], in_=sin1.rearrange("(p i) c -> p i c", i=GROUPS1))
        nc.sync.dma_start(out=cos_raw[:, GROUPS1, :], in_=cos2)
        nc.sync.dma_start(out=sin_raw[:, GROUPS1, :], in_=sin2)
        load_x(0, 0)
        load_x(0, 1)
        load_w(WQ1, 0, 1, "raw_wq1")
        nc.vector.memset(bias_rows[:], 0.0)
        for m in range(len(weights)):
            rows = bias_rows[PAIRS * m : PAIRS * (m + 1), :]
            nc.sync.dma_start(out=rows, in_=biases[m].rearrange("(r c) -> r c", c=PAIR))
        for pair in range(1, PAIRS - 1):
            load_w(WQ1, pair, 1, "raw_wq1")
        load_x(1, 0)
        load_w(WQ1, PAIRS - 1, 1, "raw_wq1")
        load_x(1, 1)
        load_x(2, 0)
        load_x(2, 1)
        load_w(*later_pairs[0], 2, "raw")
        make_identity(nc, ident_f32[:])
        nc.vector.tensor_copy(out=ident_bf16[:], in_=ident_f32[:])

        spread_tables()
        for hb in range(2):
            for g in range(PASSES):
                turn_x(0, g, 2 * hb, 2 * hb + 2)
        for g in range(PASSES):
            group_w(WQ1, 0, g, nc.vector.tensor_copy)
        quantize_x(0, 0)
        quantize_w(WQ1, 0, 0, PASSES)
        quantize_x(0, 1)
        turn_bias()
        turn_tables(0)
        multiply(0)
        for g in range(PASSES):
            group_w(WQ1, 1, g, nc.vector.tensor_copy)
        for g in range(PASSES):
            group_w(WQ1, 2, g, nc.scalar.copy)
        quantize_w(WQ1, 1, 0, PASSES)
        for g in range(PASSES):
            group_w(WQ1, 3, g, nc.scalar.copy)
        for g in range(PASSES):
            turn_x(1, g, 0, 2)

        x_turns = {0: [(1, g, 2, B) for g in range(PASSES)]}
        x_quantize = {1 + g: (1, g) for g in range(PASSES)}
        for i, slot0, batches in ((2, X2_SLOT, 2), (3, X3_SLOT, 1)):
            steps = B // batches
            for g in range(PASSES):
                for s in range(steps):
                    x_turns[slot0 + steps * g + s] = [(i, g, batches * s, batches * (s + 1))]
                x_quantize[slot0 + steps * (g + 1) - 1 + QUANTIZE_X_LAG] = (i, g)
        unit_groups = [unit[2] for unit in units]
        table_turns = {0: 1, **{unit_groups.index(i) - TABLE_LEAD: i for i in range(2, GROUPS)}}
        w_loads = {2 * n: later_pairs[n + 2] for n in range(0, len(later_pairs) - 2, 2)}

        for n in range(last + 1):
            if n < last:
                multiply(n + 1)
            for job in x_turns.get(n, []):
                turn_x(*job)
            if n in table_turns:
                turn_tables(table_turns[n])
            if n > 0:
                done = n - 1
                for s in range(GPSIMD_PLACES, 2 * B):
                    turn_out(done, s % B, s // B, terms(done, 0, s % B, s // B))
                for hb in (1, 0):
                    for s in range(GPSIMD_PLACES):
                        if s % B // 2 == hb:
                            turn_out(done, s % B, s // B, [added[done][:, s, :]])
                    copy_out(done, hb)
                if units[done][2] >= GROUPS1 - 1:
                    store(done, 0, B)
            if 0 <= n - GROUP_W_SLOT < len(later_passes):
                group_w(*later_passes[n - GROUP_W_SLOT], nc.scalar.copy)
            if n in w_loads:
                load_w(*w_loads[n], 2, "raw")
            if n == 0:
                load_x(GROUPS1, 0)
                load_x(GROUPS1, 1)
            if n < last:
                rotate(n, 0, 0, B)
                rotate(n, 1, 0, B)
                if n + 2 < PAIRS:
                    quantize_w(WQ1, n + 2, 0, PASSES)
                if n in x_quantize:
                    quantize_x(*x_quantize[n])
                if 0 <= n - GROUP_W_SLOT - QUANTIZE_W_LAG < len(later_passes):
                    m, pair, g = later_passes[n - GROUP_W_SLOT - QUANTIZE_W_LAG]
                    quantize_w(m, pair, g, g + 1)
                add_terms(n)

        for hb in range(2):
            b0, b1 = 2 * hb, 2 * hb + 2
            rotate(last, 0, b0, b1)
            rotate(last, 1, b0, b1)
            for b in range(b0, b1):
                for e in range(2):
                    turn_out(last, b, e, terms(last, b0, b, e))
            copy_out(last, hb)
            store(last, b0, b1)
